import numpy as np
import ml_dtypes


def mxq(x, axis, fmt="e4m3"):
    dtype, down = {"e4m3": (ml_dtypes.float8_e4m3fn, 7), "e5m2": (ml_dtypes.float8_e5m2, 14)}[fmt]
    v = np.moveaxis(np.asarray(x, np.float32).astype(ml_dtypes.bfloat16).astype(np.float64), axis, -1)
    blocks = v.reshape(v.shape[:-1] + (-1, 32))
    amax = np.abs(blocks).max(-1, keepdims=True)
    byte = np.maximum(np.where(amax > 0, np.frexp(amax)[1] - 1 + 127, 0) - down, 1)
    scale = np.exp2(byte - 127.0)
    codes = (blocks / scale).astype(np.float32).astype(dtype).astype(np.float64)
    return np.moveaxis((codes * scale).reshape(v.shape), -1, axis)


WIDE = False


def mx_kscale(k):
    if not WIDE:
        return np.ones(k)
    levels = np.array([10, -10, 5, -5, 0])
    if k % 512:
        return np.exp2(np.random.permutation(np.resize(levels, k // 32))).repeat(32)
    a = np.empty((k // 512, 16))
    for p in range(k // 512):
        a[p, :8] = np.random.permutation(np.resize(levels, 8))
        for g in range(8):
            far = levels[np.abs(levels - a[p, g]) >= 10]
            a[p, g + 8] = far[np.random.randint(len(far))]
    return np.exp2(a.ravel()).repeat(32)


BF16 = ml_dtypes.bfloat16


def bf(x):
    return np.asarray(x, np.float32).astype(BF16)


def f64(x):
    return np.asarray(x).astype(np.float64)


M, N, NFEAT, NHID, NCLASS = 4096, 4096, 2048, 2048, 8
ADJ_P = 0.01
SIG = 4.5


def setup_inputs():
    s = mx_kscale(NHID)
    t = mx_kscale(NHID)
    c = np.sqrt(2.0 * SIG / np.sqrt(NHID)) / np.sqrt(NHID)
    return {"h": bf(np.maximum(np.random.standard_normal((N, NHID)), 0.0) * s[None, :]),
            "adj": bf(np.random.uniform(size=(N, N)) < ADJ_P),
            "Qw": bf(np.random.standard_normal((NHID, NHID)) * c / s[:, None] * t[None, :]),
            "Qb": bf(np.random.standard_normal(NHID) * 0.1 * t),
            "Kw": bf(np.random.standard_normal((NHID, NHID)) * c / s[:, None] / t[None, :]),
            "Kb": bf(np.random.standard_normal(NHID) * 0.1 / t)}


def reference(h, adj, Qw, Qb, Kw, Kb):
    hq = mxq(f64(h), 1, "e4m3")
    q = (hq @ mxq(f64(Qw), 0, "e4m3")) + f64(Qb)
    k = (hq @ mxq(f64(Kw), 0, "e4m3")) + f64(Kb)
    sc = f64(adj) * (mxq(q, 1, "e4m3") @ mxq(k, 1, "e4m3").T)
    e = np.exp(sc - sc.max(axis=1, keepdims=True))
    return e / e.sum(axis=1, keepdims=True)

@@ -1,0 +1,418 @@
+from contextlib import ExitStack
+
+import concourse.mybir as mybir
+from concourse.masks import make_identity
+
+F32 = mybir.dt.float32
+BF16 = mybir.dt.bfloat16
+U32 = mybir.dt.uint32
+U8 = mybir.dt.uint8
+FP8X4 = mybir.dt.float8_e4m3fn_x4
+ACT = mybir.ActivationFunctionType
+ALU = mybir.AluOpType
+AX = mybir.AxisListType
+
+P = 128
+N_TOK = 4096
+D = 2048
+NB = 8
+FLOPS = 2 * 2 * N_TOK * D * D + 2 * N_TOK * N_TOK * D
+
+W_SLOT = [0, 1, 2, 3, 4, 5, 0, 1]
+
+
+def tile_gtransformerblock_pb_l_kernel(tc, h, adj, Qw, Qb, Kw, Kb, out):
+    nc = tc.nc
+    pending = {}
+    now = [0]
+    counts = {"bank": 0, "grp": 0, "hg": 0, "raw": 0, "st": 0}
+
+    def later(lag, fn):
+        key = now[0] + lag
+        lst = pending.get(key)
+        if lst is None:
+            lst = []
+            pending[key] = lst
+        lst.append(fn)
+
+    def tick():
+        while now[0] in pending:
+            for fn in pending.pop(now[0]):
+                fn()
+        now[0] += 1
+
+    def flush():
+        while len(pending) > 0:
+            tick()
+
+    def bump(what, modulo):
+        c = counts[what]
+        counts[what] = c + 1
+        return c % modulo
+
+    with ExitStack() as ctx:
+        ctx.enter_context(tc.manual_schedule())
+        keep = ctx.enter_context(tc.tile_pool(name="keep", bufs=1))
+        psum = ctx.enter_context(tc.psum_pool(name="psum", bufs=1))
+
+        def new_bank(shape):
+            return psum.tile(shape, F32, name="bank", tag="bank%d" % bump("bank", 8))
+
+        def code_tile(slot):
+            codes = keep.tile([P, 4, 512], U32, name="wc", tag="wc%d" % slot, align_bytes=64)
+            scales = keep.tile([P, 512], U8, name="ws", tag="ws%d" % slot, align_bytes=64)
+            return (codes, scales)
+
+        kc = []
+        for G in range(4):
+            kc.append(keep.tile([P, N_TOK], U32, name="kc%d" % G, tag="kc%d" % G, align_bytes=64))
+        ks = keep.tile([P, N_TOK], U8, name="ks", tag="ks", align_bytes=64)
+        hc = []
+        hs = []
+        for b in range(NB):
+            hc.append(keep.tile([P, 4, 512], U32, name="hc%d" % b, tag="h%d" % b, align_bytes=64))
+            hs.append(keep.tile([P, 512], U8, name="hs%d" % b, tag="hs%d" % b, align_bytes=64))
+        wt = {}
+        for n in range(6):
+            wt[n] = code_tile(W_SLOT[n])
+        kb32 = keep.tile([P, 16], F32, name="kb32", tag="kb32")
+        qb32 = keep.tile([P, 16], F32, name="qb32", tag="qb32")
+        qt = {}
+        adj_t = {}
+
+        def proj_job(w, b, t, raw, bias_col):
+            wcodes, wscales = w
+            bank = new_bank([P, 512])
+            for g in range(4):
+                nc.tensor.matmul_mx(
+                    out=bank[:],
+                    lhsT=wcodes[:, g, t * P : (t + 1) * P].bitcast(FP8X4),
+                    lhsT_scale=wscales[4 * g :, t * P : (t + 1) * P],
+                    rhs=hc[b][:, g, :].bitcast(FP8X4),
+                    rhs_scale=hs[b][4 * g :, :],
+                    start=(g == 0),
+                    stop=(g == 3),
+                )
+            later(
+                1,
+                lambda: nc.scalar.activation(
+                    out=raw[:, t, :], in_=bank[:], func=ACT.Identity, bias=bias_col, scale=1.0
+                ),
+            )
+            tick()
+
+        with tc.tile_pool(name="stage1", bufs=1) as st1:
+            ident = st1.tile([P, P], F32, name="ident", tag="ident")
+            make_identity(nc, ident[:])
+            warm = st1.tile([P, 1], F32, name="warm", tag="warm")
+            warm2 = st1.tile([P, 1], F32, name="warm2", tag="warm2")
+            nc.vector.memset(warm[:], 0.0)
+            nc.scalar.activation(out=warm2[:], in_=warm[:], func=ACT.Exp)
+            kb16 = st1.tile([P, 4, 4], BF16, name="kb16", tag="kb16")
+            qb16 = st1.tile([P, 4, 4], BF16, name="qb16", tag="qb16")
+            nc.scalar.dma_start(out=kb16[:], in_=Kb.rearrange("(g p t) -> p g t", p=P, t=4))
+            nc.scalar.dma_start(out=qb16[:], in_=Qb.rearrange("(g p t) -> p g t", p=P, t=4))
+
+            hraw = {}
+            wraw = {}
+
+            def load_h(b, half):
+                if b >= NB:
+                    return
+                for rr in range(2):
+                    rt = 4 * b + 2 * half + rr
+                    t = st1.tile([P, D], BF16, name="hraw", tag="hraw%d" % (2 * half + rr))
+                    nc.sync.dma_start(out=t[:], in_=h[rt * P : (rt + 1) * P, :])
+                    hraw[(b, half, rr)] = t
+
+            def new_group():
+                return st1.tile([P, 2048], BF16, name="grp", tag="grp%d" % bump("grp", 3), align_bytes=64)
+
+            def w_load(w):
+                if w >= 32:
+                    return
+                src = Kw if w < 16 else Qw
+                G = (w // 4) % 4
+                g = w % 4
+                t = st1.tile([P, 4, 512], BF16, name="wraw", tag="wraw%d" % (w % 2))
+                nc.sync.dma_start(
+                    out=t[:],
+                    in_=src[512 * g : 512 * (g + 1), 512 * G : 512 * (G + 1)].rearrange("(p j) c -> p j c", j=4),
+                )
+                wraw[w] = t
+
+            def w_copy(w, on_scalar):
+                grp = new_group()
+                dst = grp[:].rearrange("p (t m j) -> p t m j", t=4, j=4)
+                src = wraw.pop(w)[:].rearrange("p j (m t) -> p t m j", t=4)
+                if on_scalar:
+                    nc.scalar.copy(out=dst, in_=src)
+                else:
+                    nc.vector.tensor_copy(out=dst, in_=src)
+                w_load(w + 2)
+                return grp
+
+            def w_quant(w, grp):
+                n = w // 4
+                g = w % 4
+                if g == 0 and n >= 6:
+                    wt[n] = code_tile(W_SLOT[n])
+                codes, scales = wt[n]
+                nc.vector.quantize_mx(
+                    out=codes[:, g, :].bitcast(FP8X4), scales=scales[4 * g :, :], in_=grp[:]
+                )
+
+            def quant_h(b, half, g, hg):
+                nc.vector.quantize_mx(
+                    out=hc[b][:, g, 256 * half : 256 * (half + 1)].bitcast(FP8X4),
+                    scales=hs[b][4 * g :, 256 * half : 256 * (half + 1)],
+                    in_=hg[:].rearrange("p r j -> p (r j)"),
+                )
+
+            def evac_h(b, half, g, xt):
+                hg = st1.tile([P, 256, 4], BF16, name="hg", tag="hg%d" % bump("hg", 2), align_bytes=64)
+                nc.scalar.copy(out=hg[:].bitcast(F32), in_=xt[:].rearrange("p u r -> p r u"))
+                later(1, lambda: quant_h(b, half, g, hg))
+
+            def bank_of_transposes(b, half, g):
+                xt = new_bank([P, 2, 256])
+                for rr in range(2):
+                    words = hraw[(b, half, rr)][:].bitcast(F32)
+                    for u in range(2):
+                        nc.tensor.transpose(
+                            xt[:, u, rr * P : (rr + 1) * P],
+                            words[:, 256 * g + u : 256 * (g + 1) : 2],
+                            ident[:],
+                        )
+                later(1, lambda: evac_h(b, half, g, xt))
+                tick()
+
+            def transposes(b, half):
+                if b >= NB:
+                    return
+                for g in range(4):
+                    bank_of_transposes(b, half, g)
+                load_h(b + 1, half)
+
+            def finish_unit1(raw, codes_ap, scales_ap, w):
+                def step1():
+                    grp = new_group()
+                    nc.vector.tensor_copy(
+                        out=grp[:].rearrange("p (n t) -> p n t", t=4), in_=raw[:].rearrange("p t n -> p n t")
+                    )
+                    later(1, lambda: nc.vector.quantize_mx(out=codes_ap, scales=scales_ap, in_=grp[:]))
+                    if w < 32:
+                        on_scalar = (w >= 12) and (w % 2 == 1)
+                        wgrp = w_copy(w, on_scalar)
+                        later(3 if on_scalar else 1, lambda: w_quant(w, wgrp))
+
+                later(1, step1)
+
+            def new_raw1():
+                return st1.tile([P, 4, 512], BF16, name="raw", tag="raw%d" % bump("raw", 2))
+
+            load_h(0, 0)
+            w_load(0)
+            w_load(1)
+            load_h(0, 1)
+            g0 = w_copy(0, False)
+            g1 = w_copy(1, False)
+            w_quant(0, g0)
+            transposes(0, 0)
+            w_quant(1, g1)
+            transposes(0, 1)
+            flush()
+            g2 = w_copy(2, False)
+            g3 = w_copy(3, True)
+            w_quant(2, g2)
+            nc.vector.tensor_copy(out=kb32[:], in_=kb16[:].rearrange("p g t -> p (g t)"))
+            nc.vector.tensor_copy(out=qb32[:], in_=qb16[:].rearrange("p g t -> p (g t)"))
+            w_quant(3, g3)
+
+            unit = 0
+            for n in range(5):
+                for b in range(NB if n < 4 else 1):
+                    for G in range(4 if n == 4 else 1):
+                        raw = new_raw1()
+                        if n < 4:
+                            w = wt[n]
+                            bias = kb32
+                            Gc = n
+                        else:
+                            w = wt[4 + G]
+                            bias = qb32
+                            Gc = G
+                        for t in range(4):
+                            if n == 0 and t % 2 == 0:
+                                transposes(b + 1, t // 2)
+                            proj_job(w, b, t, raw, bias[:, 4 * Gc + t : 4 * Gc + t + 1])
+                        if n < 4:
+                            codes_ap = kc[n][:, 512 * b : 512 * (b + 1)].bitcast(FP8X4)
+                            scales_ap = ks[4 * n :, 512 * b : 512 * (b + 1)]
+                        else:
+                            if G == 0:
+                                qt[0] = code_tile(2)
+                            codes_ap = qt[0][0][:, G, :].bitcast(FP8X4)
+                            scales_ap = qt[0][1][4 * G :, :]
+                        finish_unit1(raw, codes_ap, scales_ap, 4 + unit)
+                        unit += 1
+            adj_t[0] = keep.tile([P, N_TOK], BF16, name="adj", tag="h0", align_bytes=64)
+            nc.sync.dma_start(out=adj_t[0][:], in_=adj[0:P, :])
+            flush()
+
+        with tc.tile_pool(name="stage2", bufs=1) as st2:
+            efree = [(st2, "e0"), (st2, "e1"), (st2, "e2"), (st2, "e3")]
+            row_e = {}
+            stats = {}
+
+            def load_adj(i):
+                if i >= 32:
+                    return
+                if i % 2 == 0:
+                    t = keep.tile([P, N_TOK], BF16, name="adj", tag="h0", align_bytes=64)
+                else:
+                    t = st2.tile([P, N_TOK], BF16, name="adjx", tag="adjx", align_bytes=64)
+                nc.sync.dma_start(out=t[:], in_=adj[i * P : (i + 1) * P, :])
+                adj_t[i] = t
+
+            def new_e():
+                slot = efree.pop(0)
+                efree.append(slot)
+                return slot[0].tile([P, 2, 1024], F32, name="e", tag=slot[1], align_bytes=64)
+
+            def new_stats():
+                k = bump("st", 3)
+                d = {}
+                for nm_, width in (("nm", 4), ("z", 4), ("f", 4), ("fz", 4), ("nM", 1), ("Z", 1), ("r", 1)):
+                    d[nm_] = st2.tile([P, width], F32, name=nm_, tag="%s%d" % (nm_, k))
+                return d
+
+            def row_scale(i):
+                s = stats[i]
+                nc.vector.reciprocal(out=s["r"][:], in_=s["Z"][:])
+                for c in range(4):
+                    e = row_e[(i, c // 2)]
+                    nc.gpsimd.tensor_scalar(
+                        out=e[:, c % 2, :],
+                        in0=e[:, c % 2, :],
+                        scalar1=s["f"][:, c : c + 1],
+                        scalar2=s["r"][:, 0:1],
+                        op0=ALU.mult,
+                        op1=ALU.mult,
+                    )
+                    if c % 2 == 1:
+                        hh = c // 2
+                        nc.sync.dma_start(
+                            out=out[i * P : (i + 1) * P, 2048 * hh : 2048 * (hh + 1)],
+                            in_=e[:].rearrange("p a n -> p (a n)"),
+                        )
+
+            def row_sum(i):
+                s = stats[i]
+                nc.vector.scalar_tensor_tensor(
+                    out=s["fz"][:],
+                    in0=s["f"][:],
+                    scalar=1.0,
+                    in1=s["z"][:],
+                    op0=ALU.mult,
+                    op1=ALU.mult,
+                    accum_out=s["Z"][:, 0:1],
+                )
+                later(1, lambda: row_scale(i))
+
+            def row_min(i):
+                s = stats[i]
+                nc.vector.tensor_reduce(out=s["nM"][:], in_=s["nm"][:], axis=AX.X, op=ALU.min)
+                nc.scalar.activation(out=s["f"][:], in_=s["nm"][:], func=ACT.Exp, bias=s["nM"][:, 0:1], scale=-1.0)
+                later(1, lambda: row_sum(i))
+
+            def chunk_min(i, c):
+                s = stats[i]
+                e = row_e[(i, c // 2)][:, c % 2, :]
+                nc.vector.tensor_reduce(out=s["nm"][:, c : c + 1], in_=e, axis=AX.X, op=ALU.min)
+                nc.scalar.activation(
+                    out=e, in_=e, func=ACT.Exp, bias=s["nm"][:, c : c + 1], scale=-1.0, accum_out=s["z"][:, c : c + 1]
+                )
+                if c == 3:
+                    later(1, lambda: row_min(i))
+
+            def mask(i, j, bank):
+                if j == 0:
+                    stats[i] = new_stats()
+                if j % 4 == 0:
+                    row_e[(i, j // 4)] = new_e()
+                e = row_e[(i, j // 4)]
+                nc.vector.scalar_tensor_tensor(
+                    out=e[:, (j // 2) % 2, (j % 2) * 512 : (j % 2) * 512 + 512],
+                    in0=bank[:],
+                    scalar=-1.0,
+                    in1=adj_t[i][:, j * 512 : (j + 1) * 512],
+                    op0=ALU.mult,
+                    op1=ALU.mult,
+                )
+                if j == 7:
+                    load_adj(i + 2)
+                if j % 2 == 1:
+                    later(1, lambda: chunk_min(i, j // 2))
+
+            def score_job(i, j):
+                b = i // 4
+                r = i % 4
+                qcodes, qscales = qt[b]
+                bank = new_bank([P, 512])
+                for G in range(4):
+                    nc.tensor.matmul_mx(
+                        out=bank[:],
+                        lhsT=qcodes[:, G, r * P : (r + 1) * P].bitcast(FP8X4),
+                        lhsT_scale=qscales[4 * G :, r * P : (r + 1) * P],
+                        rhs=kc[G][:, j * 512 : (j + 1) * 512].bitcast(FP8X4),
+                        rhs_scale=ks[4 * G :, j * 512 : (j + 1) * 512],
+                        start=(G == 0),
+                        stop=(G == 3),
+                    )
+                later(1, lambda: mask(i, j, bank))
+                tick()
+
+            def finish_unit2(raw, codes_ap, scales_ap):
+                def step2(grp):
+                    nc.vector.quantize_mx(out=codes_ap, scales=scales_ap, in_=grp[:])
+
+                def step1():
+                    grp = st2.tile([P, 2048], BF16, name="og", tag="og", align_bytes=64)
+                    nc.scalar.copy(
+                        out=grp[:].rearrange("p (n t) -> p n t", t=4), in_=raw[:].rearrange("p t n -> p n t")
+                    )
+                    later(4, lambda: step2(grp))
+
+                later(1, step1)
+
+            load_adj(1)
+            qraw = {}
+            for b in range(NB):
+                if b >= 1:
+                    efree.insert(0, (keep, "h%d" % b))
+                todo = []
+                if b + 1 < NB:
+                    for G in range(4):
+                        for t in range(4):
+                            todo.append((G, t))
+                for s in range(32):
+                    n_q = 0
+                    if s == 0:
+                        n_q = 4
+                    elif s % 2 == 0 and s <= 24:
+                        n_q = 1
+                    for k in range(n_q):
+                        if len(todo) > 0:
+                            G, t = todo.pop(0)
+                            if G == 0 and t == 0:
+                                qt[b + 1] = code_tile(2 + (b + 1) % 2)
+                            if t == 0:
+                                qraw[0] = st2.tile([P, 4, 512], BF16, name="qraw", tag="qraw")
+                            proj_job(wt[4 + G], b + 1, t, qraw[0], qb32[:, 4 * G + t : 4 * G + t + 1])
+                            if t == 3:
+                                finish_unit2(
+                                    qraw[0], qt[b + 1][0][:, G, :].bitcast(FP8X4), qt[b + 1][1][4 * G :, :]
+                                )
+                    score_job(4 * b + s // 8, s % 8)
+            flush()

@@ -61,7 +61,7 @@ def tile_gtransformerblock_pb_l_kernel(tc, h, adj, Qw, Qb, Kw, Kb, out):
         def code_tile(slot):
             codes = keep.tile([P, 4, 512], U32, name="wc", tag="wc%d" % slot, align_bytes=64)
             scales = keep.tile([P, 512], U8, name="ws", tag="ws%d" % slot, align_bytes=64)
-            return (codes, scales)
+            return (codes, [scales, scales, scales, scales])
 
         kc = []
         for G in range(4):
@@ -87,7 +87,7 @@ def tile_gtransformerblock_pb_l_kernel(tc, h, adj, Qw, Qb, Kw, Kb, out):
                 nc.tensor.matmul_mx(
                     out=bank[:],
                     lhsT=wcodes[:, g, t * P : (t + 1) * P].bitcast(FP8X4),
-                    lhsT_scale=wscales[4 * g :, t * P : (t + 1) * P],
+                    lhsT_scale=wscales[g][4 * g :, t * P : (t + 1) * P],
                     rhs=hc[b][:, g, :].bitcast(FP8X4),
                     rhs_scale=hs[b][4 * g :, :],
                     start=(g == 0),
@@ -106,6 +106,8 @@ def tile_gtransformerblock_pb_l_kernel(tc, h, adj, Qw, Qb, Kw, Kb, out):
             make_identity(nc, ident[:])
             warm = st1.tile([P, 1], F32, name="warm", tag="warm")
             warm2 = st1.tile([P, 1], F32, name="warm2", tag="warm2")
+            zeros = st1.tile([P, 512], BF16, name="zeros", tag="zeros")
+            nc.vector.memset(zeros[:], 0.0)
             nc.vector.memset(warm[:], 0.0)
             nc.scalar.activation(out=warm2[:], in_=warm[:], func=ACT.Exp)
             kb16 = st1.tile([P, 4, 4], BF16, name="kb16", tag="kb16")
@@ -125,6 +127,9 @@ def tile_gtransformerblock_pb_l_kernel(tc, h, adj, Qw, Qb, Kw, Kb, out):
                     nc.sync.dma_start(out=t[:], in_=h[rt * P : (rt + 1) * P, :])
                     hraw[(b, half, rr)] = t
 
+            def new_raw1():
+                return st1.tile([P, 4, 512], BF16, name="raw", tag="raw%d" % bump("raw", 2))
+
             def new_group():
                 return st1.tile([P, 2048], BF16, name="grp", tag="grp%d" % bump("grp", 3), align_bytes=64)
 
@@ -134,7 +139,10 @@ def tile_gtransformerblock_pb_l_kernel(tc, h, adj, Qw, Qb, Kw, Kb, out):
                 src = Kw if w < 16 else Qw
                 G = (w // 4) % 4
                 g = w % 4
-                t = st1.tile([P, 4, 512], BF16, name="wraw", tag="wraw%d" % (w % 2))
+                if w == 2 or w == 3:
+                    t = new_raw1()
+                else:
+                    t = st1.tile([P, 4, 512], BF16, name="wraw", tag="wraw%d" % (w % 2))
                 nc.sync.dma_start(
                     out=t[:],
                     in_=src[512 * g : 512 * (g + 1), 512 * G : 512 * (G + 1)].rearrange("(p j) c -> p j c", j=4),
@@ -149,7 +157,8 @@ def tile_gtransformerblock_pb_l_kernel(tc, h, adj, Qw, Qb, Kw, Kb, out):
                     nc.scalar.copy(out=dst, in_=src)
                 else:
                     nc.vector.tensor_copy(out=dst, in_=src)
-                w_load(w + 2)
+                if w >= 2:
+                    w_load(w + 2)
                 return grp
 
             def w_quant(w, grp):
@@ -159,7 +168,7 @@ def tile_gtransformerblock_pb_l_kernel(tc, h, adj, Qw, Qb, Kw, Kb, out):
                     wt[n] = code_tile(W_SLOT[n])
                 codes, scales = wt[n]
                 nc.vector.quantize_mx(
-                    out=codes[:, g, :].bitcast(FP8X4), scales=scales[4 * g :, :], in_=grp[:]
+                    out=codes[:, g, :].bitcast(FP8X4), scales=scales[g][4 * g :, :], in_=grp[:]
                 )
 
             def quant_h(b, half, g, hg):
@@ -169,12 +178,16 @@ def tile_gtransformerblock_pb_l_kernel(tc, h, adj, Qw, Qb, Kw, Kb, out):
                     in_=hg[:].rearrange("p r j -> p (r j)"),
                 )
 
-            def evac_h(b, half, g, xt):
+            def evac_now(xt):
                 hg = st1.tile([P, 256, 4], BF16, name="hg", tag="hg%d" % bump("hg", 2), align_bytes=64)
                 nc.scalar.copy(out=hg[:].bitcast(F32), in_=xt[:].rearrange("p u r -> p r u"))
+                return hg
+
+            def evac_h(b, half, g, xt):
+                hg = evac_now(xt)
                 later(1, lambda: quant_h(b, half, g, hg))
 
-            def bank_of_transposes(b, half, g):
+            def t_bank(b, half, g):
                 xt = new_bank([P, 2, 256])
                 for rr in range(2):
                     words = hraw[(b, half, rr)][:].bitcast(F32)
@@ -184,8 +197,17 @@ def tile_gtransformerblock_pb_l_kernel(tc, h, adj, Qw, Qb, Kw, Kb, out):
                             words[:, 256 * g + u : 256 * (g + 1) : 2],
                             ident[:],
                         )
+                return xt
+
+            def bank_of_transposes(b, half, g):
+                xt = t_bank(b, half, g)
                 later(1, lambda: evac_h(b, half, g, xt))
                 tick()
+
+            def dummies(n):
+                bank = new_bank([P, 512])
+                for k in range(n):
+                    nc.tensor.matmul(out=bank[:], lhsT=zeros[:, 0:P], rhs=zeros[:], start=True, stop=True)
 
             def transposes(b, half):
                 if b >= NB:
@@ -208,31 +230,79 @@ def tile_gtransformerblock_pb_l_kernel(tc, h, adj, Qw, Qb, Kw, Kb, out):
 
                 later(1, step1)
 
-            def new_raw1():
-                return st1.tile([P, 4, 512], BF16, name="raw", tag="raw%d" % bump("raw", 2))
-
+            for g in range(1, 4):
+                wt[0][1][g] = st1.tile([P, 512], U8, name="k0s", tag="k0s%d" % g, align_bytes=64)
             load_h(0, 0)
-            w_load(0)
-            w_load(1)
             load_h(0, 1)
+            for w in range(4):
+                w_load(w)
+            dummies(8)
+            xa = []
+            for g in range(4):
+                xa.append(t_bank(0, 0, g))
+            load_h(1, 0)
+            dummies(2)
+            xb = []
+            for g in range(4):
+                xb.append(t_bank(0, 1, g))
+            load_h(1, 1)
+            ha0 = evac_now(xa[0])
+            ha1 = evac_now(xa[1])
+            quant_h(0, 0, 0, ha0)
+            ha2 = evac_now(xa[2])
+            quant_h(0, 0, 1, ha1)
+            ha3 = evac_now(xa[3])
+            quant_h(0, 0, 2, ha2)
+            hb0 = evac_now(xb[0])
+            quant_h(0, 0, 3, ha3)
+            hb1 = evac_now(xb[1])
             g0 = w_copy(0, False)
-            g1 = w_copy(1, False)
+            quant_h(0, 1, 0, hb0)
+            hb2 = evac_now(xb[2])
+            quant_h(0, 1, 1, hb1)
+            hb3 = evac_now(xb[3])
             w_quant(0, g0)
-            transposes(0, 0)
+            quant_h(0, 1, 2, hb2)
+            g2 = w_copy(2, True)
+            g1 = w_copy(1, False)
+            quant_h(0, 1, 3, hb3)
             w_quant(1, g1)
-            transposes(0, 1)
-            flush()
-            g2 = w_copy(2, False)
-            g3 = w_copy(3, True)
+            g3 = w_copy(3, False)
             w_quant(2, g2)
             nc.vector.tensor_copy(out=kb32[:], in_=kb16[:].rearrange("p g t -> p (g t)"))
-            nc.vector.tensor_copy(out=qb32[:], in_=qb16[:].rearrange("p g t -> p (g t)"))
             w_quant(3, g3)
+            nc.vector.tensor_copy(out=qb32[:], in_=qb16[:].rearrange("p g t -> p (g t)"))
+
+            raw = new_raw1()
+            first = []
+            for t in range(4):
+                first.append(new_bank([P, 512]))
+            for g in range(4):
+                for t in range(4):
+                    nc.tensor.matmul_mx(
+                        out=first[t][:],
+                        lhsT=wt[0][0][:, g, t * P : (t + 1) * P].bitcast(FP8X4),
+                        lhsT_scale=wt[0][1][g][4 * g :, t * P : (t + 1) * P],
+                        rhs=hc[0][:, g, :].bitcast(FP8X4),
+                        rhs_scale=hs[0][4 * g :, :],
+                        start=(g == 0),
+                        stop=(g == 3),
+                    )
+            for t in range(4):
+                nc.scalar.activation(
+                    out=raw[:, t, :], in_=first[t][:], func=ACT.Identity, bias=kb32[:, t : t + 1], scale=1.0
+                )
+            transposes(1, 0)
+            transposes(1, 1)
+            finish_unit1(raw, kc[0][:, 0:512].bitcast(FP8X4), ks[0:, 0:512], 4)
 
             unit = 0
             for n in range(5):
                 for b in range(NB if n < 4 else 1):
                     for G in range(4 if n == 4 else 1):
+                        if unit == 0:
+                            unit = 1
+                            continue
                         raw = new_raw1()
                         if n < 4:
                             w = wt[n]
@@ -253,7 +323,7 @@ def tile_gtransformerblock_pb_l_kernel(tc, h, adj, Qw, Qb, Kw, Kb, out):
                             if G == 0:
                                 qt[0] = code_tile(2)
                             codes_ap = qt[0][0][:, G, :].bitcast(FP8X4)
-                            scales_ap = qt[0][1][4 * G :, :]
+                            scales_ap = qt[0][1][G][4 * G :, :]
                         finish_unit1(raw, codes_ap, scales_ap, 4 + unit)
                         unit += 1
             adj_t[0] = keep.tile([P, N_TOK], BF16, name="adj", tag="h0", align_bytes=64)
@@ -278,42 +348,56 @@ def tile_gtransformerblock_pb_l_kernel(tc, h, adj, Qw, Qb, Kw, Kb, out):
             def new_e():
                 slot = efree.pop(0)
                 efree.append(slot)
-                return slot[0].tile([P, 2, 1024], F32, name="e", tag=slot[1], align_bytes=64)
+                return slot[0].tile([P, 2048], F32, name="e", tag=slot[1], align_bytes=64)
+
+            def chunks_of(i):
+                if i == 31:
+                    return [(0, 1024), (1024, 1024), (2048, 1024), (3072, 512), (3584, 512)]
+                return [(0, 1024), (1024, 1024), (2048, 1024), (3072, 1024)]
+
+            def chunk_ap(i, c):
+                lo, width = chunks_of(i)[c]
+                return row_e[(i, lo // 2048)][:, lo % 2048 : lo % 2048 + width]
 
             def new_stats():
                 k = bump("st", 3)
                 d = {}
-                for nm_, width in (("nm", 4), ("z", 4), ("f", 4), ("fz", 4), ("nM", 1), ("Z", 1), ("r", 1)):
+                for nm_, width in (("nm", 5), ("z", 5), ("f", 5), ("fz", 5), ("nM", 1), ("Z", 1), ("r", 1)):
                     d[nm_] = st2.tile([P, width], F32, name=nm_, tag="%s%d" % (nm_, k))
                 return d
 
             def row_scale(i):
                 s = stats[i]
                 nc.vector.reciprocal(out=s["r"][:], in_=s["Z"][:])
-                for c in range(4):
-                    e = row_e[(i, c // 2)]
-                    nc.gpsimd.tensor_scalar(
-                        out=e[:, c % 2, :],
-                        in0=e[:, c % 2, :],
+                last = i == 31
+                for c in range(len(chunks_of(i))):
+                    e = chunk_ap(i, c)
+                    eng = nc.vector if (last and c < 3) else nc.gpsimd
+                    eng.tensor_scalar(
+                        out=e,
+                        in0=e,
                         scalar1=s["f"][:, c : c + 1],
                         scalar2=s["r"][:, 0:1],
                         op0=ALU.mult,
                         op1=ALU.mult,
                     )
-                    if c % 2 == 1:
+                    lo, width = chunks_of(i)[c]
+                    if last:
+                        nc.sync.dma_start(out=out[i * P : (i + 1) * P, lo : lo + width], in_=e)
+                    elif c % 2 == 1:
                         hh = c // 2
                         nc.sync.dma_start(
-                            out=out[i * P : (i + 1) * P, 2048 * hh : 2048 * (hh + 1)],
-                            in_=e[:].rearrange("p a n -> p (a n)"),
+                            out=out[i * P : (i + 1) * P, 2048 * hh : 2048 * (hh + 1)], in_=row_e[(i, hh)][:]
                         )
 
             def row_sum(i):
                 s = stats[i]
+                nch = len(chunks_of(i))
                 nc.vector.scalar_tensor_tensor(
-                    out=s["fz"][:],
-                    in0=s["f"][:],
+                    out=s["fz"][:, 0:nch],
+                    in0=s["f"][:, 0:nch],
                     scalar=1.0,
-                    in1=s["z"][:],
+                    in1=s["z"][:, 0:nch],
                     op0=ALU.mult,
                     op1=ALU.mult,
                     accum_out=s["Z"][:, 0:1],
@@ -322,18 +406,21 @@ def tile_gtransformerblock_pb_l_kernel(tc, h, adj, Qw, Qb, Kw, Kb, out):
 
             def row_min(i):
                 s = stats[i]
-                nc.vector.tensor_reduce(out=s["nM"][:], in_=s["nm"][:], axis=AX.X, op=ALU.min)
-                nc.scalar.activation(out=s["f"][:], in_=s["nm"][:], func=ACT.Exp, bias=s["nM"][:, 0:1], scale=-1.0)
+                nch = len(chunks_of(i))
+                nc.vector.tensor_reduce(out=s["nM"][:], in_=s["nm"][:, 0:nch], axis=AX.X, op=ALU.min)
+                nc.scalar.activation(
+                    out=s["f"][:, 0:nch], in_=s["nm"][:, 0:nch], func=ACT.Exp, bias=s["nM"][:, 0:1], scale=-1.0
+                )
                 later(1, lambda: row_sum(i))
 
             def chunk_min(i, c):
                 s = stats[i]
-                e = row_e[(i, c // 2)][:, c % 2, :]
+                e = chunk_ap(i, c)
                 nc.vector.tensor_reduce(out=s["nm"][:, c : c + 1], in_=e, axis=AX.X, op=ALU.min)
                 nc.scalar.activation(
                     out=e, in_=e, func=ACT.Exp, bias=s["nm"][:, c : c + 1], scale=-1.0, accum_out=s["z"][:, c : c + 1]
                 )
-                if c == 3:
+                if c == len(chunks_of(i)) - 1:
                     later(1, lambda: row_min(i))
 
             def mask(i, j, bank):
@@ -343,7 +430,7 @@ def tile_gtransformerblock_pb_l_kernel(tc, h, adj, Qw, Qb, Kw, Kb, out):
                     row_e[(i, j // 4)] = new_e()
                 e = row_e[(i, j // 4)]
                 nc.vector.scalar_tensor_tensor(
-                    out=e[:, (j // 2) % 2, (j % 2) * 512 : (j % 2) * 512 + 512],
+                    out=e[:, (j % 4) * 512 : (j % 4) * 512 + 512],
                     in0=bank[:],
                     scalar=-1.0,
                     in1=adj_t[i][:, j * 512 : (j + 1) * 512],
@@ -352,8 +439,9 @@ def tile_gtransformerblock_pb_l_kernel(tc, h, adj, Qw, Qb, Kw, Kb, out):
                 )
                 if j == 7:
                     load_adj(i + 2)
-                if j % 2 == 1:
-                    later(1, lambda: chunk_min(i, j // 2))
+                ends = [lo + width for lo, width in chunks_of(i)]
+                if (j + 1) * 512 in ends:
+                    later(1, lambda: chunk_min(i, ends.index((j + 1) * 512)))
 
             def score_job(i, j):
                 b = i // 4
@@ -364,7 +452,7 @@ def tile_gtransformerblock_pb_l_kernel(tc, h, adj, Qw, Qb, Kw, Kb, out):
                     nc.tensor.matmul_mx(
                         out=bank[:],
                         lhsT=qcodes[:, G, r * P : (r + 1) * P].bitcast(FP8X4),
-                        lhsT_scale=qscales[4 * G :, r * P : (r + 1) * P],
+                        lhsT_scale=qscales[G][4 * G :, r * P : (r + 1) * P],
                         rhs=kc[G][:, j * 512 : (j + 1) * 512].bitcast(FP8X4),
                         rhs_scale=ks[4 * G :, j * 512 : (j + 1) * 512],
                         start=(G == 0),
@@ -412,7 +500,7 @@ def tile_gtransformerblock_pb_l_kernel(tc, h, adj, Qw, Qb, Kw, Kb, out):
                             proj_job(wt[4 + G], b + 1, t, qraw[0], qb32[:, 4 * G + t : 4 * G + t + 1])
                             if t == 3:
                                 finish_unit2(
-                                    qraw[0], qt[b + 1][0][:, G, :].bitcast(FP8X4), qt[b + 1][1][4 * G :, :]
+                                    qraw[0], qt[b + 1][0][:, G, :].bitcast(FP8X4), qt[b + 1][1][G][4 * G :, :]
                                 )
                     score_job(4 * b + s // 8, s % 8)
             flush()

@@ -13,42 +13,49 @@ ALU = mybir.AluOpType
 AX = mybir.AxisListType
 
 P = 128
-N_TOK = 4096
-D = 2048
-NB = 8
-FLOPS = 2 * 2 * N_TOK * D * D + 2 * N_TOK * N_TOK * D
+TOKENS = 4096
+FEATURES = 2048
+PASSES = FEATURES // (4 * P)
+WIDE = 512
+BLOCKS = TOKENS // WIDE
+GROUPS = FEATURES // WIDE
+ROW_TILES = TOKENS // P
+BANKS = 8
 
-W_SLOT = [0, 1, 2, 3, 4, 5, 0, 1]
+FLOPS = 2 * 2 * TOKENS * FEATURES * FEATURES + 2 * TOKENS * TOKENS * FEATURES
+
+WEIGHT_PLACE = [0, 1, 2, 3, 4, 5, 0, 1]
+Q_PLACE = [2, 3]
+WEIGHT_TASKS = 2 * GROUPS * PASSES
 
 
 def tile_gtransformerblock_pb_l_kernel(tc, h, adj, Qw, Qb, Kw, Kb, out):
     nc = tc.nc
-    pending = {}
-    now = [0]
-    counts = {"bank": 0, "grp": 0, "hg": 0, "raw": 0, "st": 0}
 
-    def later(lag, fn):
-        key = now[0] + lag
-        lst = pending.get(key)
-        if lst is None:
-            lst = []
-            pending[key] = lst
-        lst.append(fn)
+    clock = [0]
+    entered = {}
+    turns = {}
+
+    def later(lag, step):
+        due = clock[0] + lag
+        if due not in entered:
+            entered[due] = []
+        entered[due].append(step)
 
     def tick():
-        while now[0] in pending:
-            for fn in pending.pop(now[0]):
-                fn()
-        now[0] += 1
+        while clock[0] in entered:
+            for step in entered.pop(clock[0]):
+                step()
+        clock[0] += 1
 
-    def flush():
-        while len(pending) > 0:
+    def run_out():
+        while len(entered) > 0:
             tick()
 
-    def bump(what, modulo):
-        c = counts[what]
-        counts[what] = c + 1
-        return c % modulo
+    def turn(family, n):
+        count = turns.get(family, 0)
+        turns[family] = count + 1
+        return "%s%d" % (family, count % n)
 
     with ExitStack() as ctx:
         ctx.enter_context(tc.manual_schedule())
@@ -56,451 +63,370 @@ def tile_gtransformerblock_pb_l_kernel(tc, h, adj, Qw, Qb, Kw, Kb, out):
         psum = ctx.enter_context(tc.psum_pool(name="psum", bufs=1))
 
         def new_bank(shape):
-            return psum.tile(shape, F32, name="bank", tag="bank%d" % bump("bank", 8))
+            return psum.tile(shape, F32, name="bank", tag=turn("bank", BANKS))
 
-        def code_tile(slot):
-            codes = keep.tile([P, 4, 512], U32, name="wc", tag="wc%d" % slot, align_bytes=64)
-            scales = keep.tile([P, 512], U8, name="ws", tag="ws%d" % slot, align_bytes=64)
-            return (codes, [scales, scales, scales, scales])
+        def codes_at(place):
+            codes = keep.tile([P, PASSES, WIDE], U32, name="codes", tag="codes%d" % place, align_bytes=64)
+            scales = keep.tile([P, WIDE], U8, name="scales", tag="scales%d" % place, align_bytes=64)
+            return (codes, scales)
 
-        kc = []
-        for G in range(4):
-            kc.append(keep.tile([P, N_TOK], U32, name="kc%d" % G, tag="kc%d" % G, align_bytes=64))
-        ks = keep.tile([P, N_TOK], U8, name="ks", tag="ks", align_bytes=64)
-        hc = []
-        hs = []
-        for b in range(NB):
-            hc.append(keep.tile([P, 4, 512], U32, name="hc%d" % b, tag="h%d" % b, align_bytes=64))
-            hs.append(keep.tile([P, 512], U8, name="hs%d" % b, tag="hs%d" % b, align_bytes=64))
-        wt = {}
+        k_codes = []
+        for c in range(GROUPS):
+            k_codes.append(keep.tile([P, TOKENS], U32, name="k_codes", tag="k_codes%d" % c, align_bytes=64))
+        k_scales = keep.tile([P, TOKENS], U8, name="k_scales", tag="k_scales", align_bytes=64)
+        h_codes = []
+        h_scales = []
+        for b in range(BLOCKS):
+            h_codes.append(keep.tile([P, PASSES, WIDE], U32, name="h_codes", tag="h%d" % b, align_bytes=64))
+            h_scales.append(keep.tile([P, WIDE], U8, name="h_scales", tag="h_scales%d" % b, align_bytes=64))
+        weights = {}
         for n in range(6):
-            wt[n] = code_tile(W_SLOT[n])
-        kb32 = keep.tile([P, 16], F32, name="kb32", tag="kb32")
-        qb32 = keep.tile([P, 16], F32, name="qb32", tag="qb32")
-        qt = {}
-        adj_t = {}
+            weights[n] = codes_at(WEIGHT_PLACE[n])
+        k_bias = keep.tile([P, GROUPS * 4], F32, name="k_bias", tag="k_bias")
+        q_bias = keep.tile([P, GROUPS * 4], F32, name="q_bias", tag="q_bias")
+        q_of_block = {}
+        adj_of_row = {}
 
-        def proj_job(w, b, t, raw, bias_col):
-            wcodes, wscales = w
-            bank = new_bank([P, 512])
-            for g in range(4):
+        def projection_job(n, b, t, raw, bias):
+            codes, scales = weights[n]
+            bank = new_bank([P, WIDE])
+            for g in range(PASSES):
                 nc.tensor.matmul_mx(
                     out=bank[:],
-                    lhsT=wcodes[:, g, t * P : (t + 1) * P].bitcast(FP8X4),
-                    lhsT_scale=wscales[g][4 * g :, t * P : (t + 1) * P],
-                    rhs=hc[b][:, g, :].bitcast(FP8X4),
-                    rhs_scale=hs[b][4 * g :, :],
+                    lhsT=codes[:, g, t * P : (t + 1) * P].bitcast(FP8X4),
+                    lhsT_scale=scales[4 * g :, t * P : (t + 1) * P],
+                    rhs=h_codes[b][:, g, :].bitcast(FP8X4),
+                    rhs_scale=h_scales[b][4 * g :, :],
                     start=(g == 0),
-                    stop=(g == 3),
+                    stop=(g == PASSES - 1),
                 )
+            column = 4 * (n % GROUPS) + t
             later(
                 1,
                 lambda: nc.scalar.activation(
-                    out=raw[:, t, :], in_=bank[:], func=ACT.Identity, bias=bias_col, scale=1.0
+                    out=raw[:, t, :], in_=bank[:], func=ACT.Identity, bias=bias[:, column : column + 1], scale=1.0
                 ),
             )
             tick()
 
-        with tc.tile_pool(name="stage1", bufs=1) as st1:
-            ident = st1.tile([P, P], F32, name="ident", tag="ident")
-            make_identity(nc, ident[:])
-            warm = st1.tile([P, 1], F32, name="warm", tag="warm")
-            warm2 = st1.tile([P, 1], F32, name="warm2", tag="warm2")
-            zeros = st1.tile([P, 512], BF16, name="zeros", tag="zeros")
-            nc.vector.memset(zeros[:], 0.0)
-            nc.vector.memset(warm[:], 0.0)
-            nc.scalar.activation(out=warm2[:], in_=warm[:], func=ACT.Exp)
-            kb16 = st1.tile([P, 4, 4], BF16, name="kb16", tag="kb16")
-            qb16 = st1.tile([P, 4, 4], BF16, name="qb16", tag="qb16")
-            nc.scalar.dma_start(out=kb16[:], in_=Kb.rearrange("(g p t) -> p g t", p=P, t=4))
-            nc.scalar.dma_start(out=qb16[:], in_=Qb.rearrange("(g p t) -> p g t", p=P, t=4))
+        with tc.tile_pool(name="phase1", bufs=1) as stage:
+            identity = stage.tile([P, P], F32, name="identity", tag="identity")
+            make_identity(nc, identity[:])
 
-            hraw = {}
-            wraw = {}
+            zero = stage.tile([P, 1], F32, name="zero", tag="zero")
+            one = stage.tile([P, 1], F32, name="one", tag="one")
+            nc.vector.memset(zero[:], 0.0)
+            nc.scalar.activation(out=one[:], in_=zero[:], func=ACT.Exp)
+
+            k_bias16 = stage.tile([P, GROUPS, 4], BF16, name="k_bias16", tag="k_bias16")
+            q_bias16 = stage.tile([P, GROUPS, 4], BF16, name="q_bias16", tag="q_bias16")
+            nc.scalar.dma_start(out=k_bias16[:], in_=Kb.rearrange("(c p t) -> p c t", p=P, t=4))
+            nc.scalar.dma_start(out=q_bias16[:], in_=Qb.rearrange("(c p t) -> p c t", p=P, t=4))
+
+            h_rows = {}
+            w_rows = {}
 
             def load_h(b, half):
-                if b >= NB:
-                    return
-                for rr in range(2):
-                    rt = 4 * b + 2 * half + rr
-                    t = st1.tile([P, D], BF16, name="hraw", tag="hraw%d" % (2 * half + rr))
-                    nc.sync.dma_start(out=t[:], in_=h[rt * P : (rt + 1) * P, :])
-                    hraw[(b, half, rr)] = t
+                if b < BLOCKS:
+                    for r in range(2):
+                        first = (4 * b + 2 * half + r) * P
+                        rows = stage.tile([P, FEATURES], BF16, name="h_rows", tag="h_rows%d" % (2 * half + r))
+                        nc.sync.dma_start(out=rows[:], in_=h[first : first + P, :])
+                        h_rows[(b, half, r)] = rows
 
-            def new_raw1():
-                return st1.tile([P, 4, 512], BF16, name="raw", tag="raw%d" % bump("raw", 2))
+            def new_grouped():
+                return stage.tile([P, 4 * WIDE], BF16, name="grouped", tag=turn("grouped", 3), align_bytes=64)
 
-            def new_group():
-                return st1.tile([P, 2048], BF16, name="grp", tag="grp%d" % bump("grp", 3), align_bytes=64)
+            def load_weights(w):
+                if w < WEIGHT_TASKS:
+                    source = Kw if w < WEIGHT_TASKS // 2 else Qw
+                    c = (w // PASSES) % GROUPS
+                    g = w % PASSES
+                    rows = stage.tile([P, 4, WIDE], BF16, name="w_rows", tag="w_rows%d" % (w % 2))
+                    nc.sync.dma_start(
+                        out=rows[:],
+                        in_=source[4 * P * g : 4 * P * (g + 1), WIDE * c : WIDE * (c + 1)].rearrange(
+                            "(p j) c -> p j c", j=4
+                        ),
+                    )
+                    w_rows[w] = rows
 
-            def w_load(w):
-                if w >= 32:
-                    return
-                src = Kw if w < 16 else Qw
-                G = (w // 4) % 4
-                g = w % 4
-                if w == 2 or w == 3:
-                    t = new_raw1()
-                else:
-                    t = st1.tile([P, 4, 512], BF16, name="wraw", tag="wraw%d" % (w % 2))
-                nc.sync.dma_start(
-                    out=t[:],
-                    in_=src[512 * g : 512 * (g + 1), 512 * G : 512 * (G + 1)].rearrange("(p j) c -> p j c", j=4),
-                )
-                wraw[w] = t
-
-            def w_copy(w, on_scalar):
-                grp = new_group()
-                dst = grp[:].rearrange("p (t m j) -> p t m j", t=4, j=4)
-                src = wraw.pop(w)[:].rearrange("p j (m t) -> p t m j", t=4)
+            def sort_weights(w, on_scalar):
+                grouped = new_grouped()
+                target = grouped[:].rearrange("p (t m j) -> p t m j", t=4, j=4)
+                source = w_rows.pop(w)[:].rearrange("p j (m t) -> p t m j", t=4)
                 if on_scalar:
-                    nc.scalar.copy(out=dst, in_=src)
+                    nc.scalar.copy(out=target, in_=source)
                 else:
-                    nc.vector.tensor_copy(out=dst, in_=src)
-                if w >= 2:
-                    w_load(w + 2)
-                return grp
+                    nc.vector.tensor_copy(out=target, in_=source)
+                load_weights(w + 2)
+                return grouped
 
-            def w_quant(w, grp):
-                n = w // 4
-                g = w % 4
-                if g == 0 and n >= 6:
-                    wt[n] = code_tile(W_SLOT[n])
-                codes, scales = wt[n]
-                nc.vector.quantize_mx(
-                    out=codes[:, g, :].bitcast(FP8X4), scales=scales[g][4 * g :, :], in_=grp[:]
-                )
+            def quantise_weights(w, grouped):
+                n = w // PASSES
+                g = w % PASSES
+                if n not in weights:
+                    weights[n] = codes_at(WEIGHT_PLACE[n])
+                codes, scales = weights[n]
+                nc.vector.quantize_mx(out=codes[:, g, :].bitcast(FP8X4), scales=scales[4 * g :, :], in_=grouped[:])
 
-            def quant_h(b, half, g, hg):
-                nc.vector.quantize_mx(
-                    out=hc[b][:, g, 256 * half : 256 * (half + 1)].bitcast(FP8X4),
-                    scales=hs[b][4 * g :, 256 * half : 256 * (half + 1)],
-                    in_=hg[:].rearrange("p r j -> p (r j)"),
-                )
-
-            def evac_now(xt):
-                hg = st1.tile([P, 256, 4], BF16, name="hg", tag="hg%d" % bump("hg", 2), align_bytes=64)
-                nc.scalar.copy(out=hg[:].bitcast(F32), in_=xt[:].rearrange("p u r -> p r u"))
-                return hg
-
-            def evac_h(b, half, g, xt):
-                hg = evac_now(xt)
-                later(1, lambda: quant_h(b, half, g, hg))
-
-            def t_bank(b, half, g):
-                xt = new_bank([P, 2, 256])
-                for rr in range(2):
-                    words = hraw[(b, half, rr)][:].bitcast(F32)
+            def transpose_job(b, half, g):
+                bank = new_bank([P, 2, 2 * P])
+                for r in range(2):
+                    words = h_rows[(b, half, r)][:].bitcast(F32)
                     for u in range(2):
                         nc.tensor.transpose(
-                            xt[:, u, rr * P : (rr + 1) * P],
-                            words[:, 256 * g + u : 256 * (g + 1) : 2],
-                            ident[:],
+                            bank[:, u, r * P : (r + 1) * P], words[:, 2 * P * g + u : 2 * P * (g + 1) : 2], identity[:]
                         )
-                return xt
 
-            def bank_of_transposes(b, half, g):
-                xt = t_bank(b, half, g)
-                later(1, lambda: evac_h(b, half, g, xt))
+                def quantise(grouped):
+                    tokens = (2 * P * half, 2 * P * (half + 1))
+                    nc.vector.quantize_mx(
+                        out=h_codes[b][:, g, tokens[0] : tokens[1]].bitcast(FP8X4),
+                        scales=h_scales[b][4 * g :, tokens[0] : tokens[1]],
+                        in_=grouped[:].rearrange("p r j -> p (r j)"),
+                    )
+
+                def empty():
+                    grouped = stage.tile([P, 2 * P, 4], BF16, name="h_grouped", tag=turn("h_grouped", 2), align_bytes=64)
+                    nc.scalar.copy(out=grouped[:].bitcast(F32), in_=bank[:].rearrange("p u r -> p r u"))
+                    later(1, lambda: quantise(grouped))
+
+                later(1, empty)
                 tick()
 
-            def dummies(n):
-                bank = new_bank([P, 512])
-                for k in range(n):
-                    nc.tensor.matmul(out=bank[:], lhsT=zeros[:, 0:P], rhs=zeros[:], start=True, stop=True)
+            def transpose_half(b, half):
+                if b < BLOCKS:
+                    for g in range(PASSES):
+                        transpose_job(b, half, g)
+                    load_h(b + 1, half)
 
-            def transposes(b, half):
-                if b >= NB:
-                    return
-                for g in range(4):
-                    bank_of_transposes(b, half, g)
-                load_h(b + 1, half)
-
-            def finish_unit1(raw, codes_ap, scales_ap, w):
-                def step1():
-                    grp = new_group()
+            def after_unit(raw, codes, scales, w):
+                def interleave():
+                    grouped = new_grouped()
                     nc.vector.tensor_copy(
-                        out=grp[:].rearrange("p (n t) -> p n t", t=4), in_=raw[:].rearrange("p t n -> p n t")
+                        out=grouped[:].rearrange("p (n t) -> p n t", t=4), in_=raw[:].rearrange("p t n -> p n t")
                     )
-                    later(1, lambda: nc.vector.quantize_mx(out=codes_ap, scales=scales_ap, in_=grp[:]))
-                    if w < 32:
-                        on_scalar = (w >= 12) and (w % 2 == 1)
-                        wgrp = w_copy(w, on_scalar)
-                        later(3 if on_scalar else 1, lambda: w_quant(w, wgrp))
+                    later(1, lambda: nc.vector.quantize_mx(out=codes, scales=scales, in_=grouped[:]))
+                    if w < WEIGHT_TASKS:
+                        on_scalar = w >= 4 + BLOCKS and w % 2 == 1
+                        w_grouped = sort_weights(w, on_scalar)
+                        later(3 if on_scalar else 1, lambda: quantise_weights(w, w_grouped))
 
-                later(1, step1)
+                later(1, interleave)
 
-            for g in range(1, 4):
-                wt[0][1][g] = st1.tile([P, 512], U8, name="k0s", tag="k0s%d" % g, align_bytes=64)
             load_h(0, 0)
+            load_weights(0)
+            load_weights(1)
             load_h(0, 1)
-            for w in range(4):
-                w_load(w)
-            dummies(8)
-            xa = []
-            for g in range(4):
-                xa.append(t_bank(0, 0, g))
-            load_h(1, 0)
-            dummies(2)
-            xb = []
-            for g in range(4):
-                xb.append(t_bank(0, 1, g))
-            load_h(1, 1)
-            ha0 = evac_now(xa[0])
-            ha1 = evac_now(xa[1])
-            quant_h(0, 0, 0, ha0)
-            ha2 = evac_now(xa[2])
-            quant_h(0, 0, 1, ha1)
-            ha3 = evac_now(xa[3])
-            quant_h(0, 0, 2, ha2)
-            hb0 = evac_now(xb[0])
-            quant_h(0, 0, 3, ha3)
-            hb1 = evac_now(xb[1])
-            g0 = w_copy(0, False)
-            quant_h(0, 1, 0, hb0)
-            hb2 = evac_now(xb[2])
-            quant_h(0, 1, 1, hb1)
-            hb3 = evac_now(xb[3])
-            w_quant(0, g0)
-            quant_h(0, 1, 2, hb2)
-            g2 = w_copy(2, True)
-            g1 = w_copy(1, False)
-            quant_h(0, 1, 3, hb3)
-            w_quant(1, g1)
-            g3 = w_copy(3, False)
-            w_quant(2, g2)
-            nc.vector.tensor_copy(out=kb32[:], in_=kb16[:].rearrange("p g t -> p (g t)"))
-            w_quant(3, g3)
-            nc.vector.tensor_copy(out=qb32[:], in_=qb16[:].rearrange("p g t -> p (g t)"))
+            for half in range(2):
+                first_grouped = sort_weights(2 * half, False)
+                second_grouped = sort_weights(2 * half + 1, False)
+                quantise_weights(2 * half, first_grouped)
+                transpose_half(0, half)
+                quantise_weights(2 * half + 1, second_grouped)
+            run_out()
+            nc.vector.tensor_copy(out=k_bias[:], in_=k_bias16[:].rearrange("p c t -> p (c t)"))
+            nc.vector.tensor_copy(out=q_bias[:], in_=q_bias16[:].rearrange("p c t -> p (c t)"))
 
-            raw = new_raw1()
-            first = []
-            for t in range(4):
-                first.append(new_bank([P, 512]))
-            for g in range(4):
+            units = []
+            for n in range(GROUPS):
+                for b in range(BLOCKS):
+                    units.append((n, b))
+            for c in range(GROUPS):
+                units.append((GROUPS + c, 0))
+            for number, (n, b) in enumerate(units):
+                raw = stage.tile([P, 4, WIDE], BF16, name="raw", tag=turn("raw", 2))
                 for t in range(4):
-                    nc.tensor.matmul_mx(
-                        out=first[t][:],
-                        lhsT=wt[0][0][:, g, t * P : (t + 1) * P].bitcast(FP8X4),
-                        lhsT_scale=wt[0][1][g][4 * g :, t * P : (t + 1) * P],
-                        rhs=hc[0][:, g, :].bitcast(FP8X4),
-                        rhs_scale=hs[0][4 * g :, :],
-                        start=(g == 0),
-                        stop=(g == 3),
-                    )
-            for t in range(4):
-                nc.scalar.activation(
-                    out=raw[:, t, :], in_=first[t][:], func=ACT.Identity, bias=kb32[:, t : t + 1], scale=1.0
-                )
-            transposes(1, 0)
-            transposes(1, 1)
-            finish_unit1(raw, kc[0][:, 0:512].bitcast(FP8X4), ks[0:, 0:512], 4)
+                    if n == 0 and t % 2 == 0:
+                        transpose_half(b + 1, t // 2)
+                    projection_job(n, b, t, raw, k_bias if n < GROUPS else q_bias)
+                if n < GROUPS:
+                    codes = k_codes[n][:, WIDE * b : WIDE * (b + 1)]
+                    scales = k_scales[4 * n :, WIDE * b : WIDE * (b + 1)]
+                else:
+                    if 0 not in q_of_block:
+                        q_of_block[0] = codes_at(Q_PLACE[0])
+                    codes = q_of_block[0][0][:, n - GROUPS, :]
+                    scales = q_of_block[0][1][4 * (n - GROUPS) :, :]
+                after_unit(raw, codes.bitcast(FP8X4), scales, 4 + number)
 
-            unit = 0
-            for n in range(5):
-                for b in range(NB if n < 4 else 1):
-                    for G in range(4 if n == 4 else 1):
-                        if unit == 0:
-                            unit = 1
-                            continue
-                        raw = new_raw1()
-                        if n < 4:
-                            w = wt[n]
-                            bias = kb32
-                            Gc = n
-                        else:
-                            w = wt[4 + G]
-                            bias = qb32
-                            Gc = G
-                        for t in range(4):
-                            if n == 0 and t % 2 == 0:
-                                transposes(b + 1, t // 2)
-                            proj_job(w, b, t, raw, bias[:, 4 * Gc + t : 4 * Gc + t + 1])
-                        if n < 4:
-                            codes_ap = kc[n][:, 512 * b : 512 * (b + 1)].bitcast(FP8X4)
-                            scales_ap = ks[4 * n :, 512 * b : 512 * (b + 1)]
-                        else:
-                            if G == 0:
-                                qt[0] = code_tile(2)
-                            codes_ap = qt[0][0][:, G, :].bitcast(FP8X4)
-                            scales_ap = qt[0][1][G][4 * G :, :]
-                        finish_unit1(raw, codes_ap, scales_ap, 4 + unit)
-                        unit += 1
-            adj_t[0] = keep.tile([P, N_TOK], BF16, name="adj", tag="h0", align_bytes=64)
-            nc.sync.dma_start(out=adj_t[0][:], in_=adj[0:P, :])
-            flush()
+            adj_of_row[0] = keep.tile([P, TOKENS], BF16, name="adj_rows", tag="h0", align_bytes=64)
+            nc.sync.dma_start(out=adj_of_row[0][:], in_=adj[0:P, :])
+            run_out()
 
-        with tc.tile_pool(name="stage2", bufs=1) as st2:
-            efree = [(st2, "e0"), (st2, "e1"), (st2, "e2"), (st2, "e3")]
-            row_e = {}
-            stats = {}
+        with tc.tile_pool(name="phase2", bufs=1) as stage:
+            half_row_places = [(stage, "half0"), (stage, "half1"), (stage, "half2"), (stage, "half3")]
+            half_rows = {}
+            stats_of_row = {}
 
             def load_adj(i):
-                if i >= 32:
-                    return
-                if i % 2 == 0:
-                    t = keep.tile([P, N_TOK], BF16, name="adj", tag="h0", align_bytes=64)
-                else:
-                    t = st2.tile([P, N_TOK], BF16, name="adjx", tag="adjx", align_bytes=64)
-                nc.sync.dma_start(out=t[:], in_=adj[i * P : (i + 1) * P, :])
-                adj_t[i] = t
+                if i < ROW_TILES:
+                    if i % 2 == 0:
+                        rows = keep.tile([P, TOKENS], BF16, name="adj_rows", tag="h0", align_bytes=64)
+                    else:
+                        rows = stage.tile([P, TOKENS], BF16, name="adj_rows", tag="adj_odd", align_bytes=64)
+                    nc.sync.dma_start(out=rows[:], in_=adj[i * P : (i + 1) * P, :])
+                    adj_of_row[i] = rows
 
-            def new_e():
-                slot = efree.pop(0)
-                efree.append(slot)
-                return slot[0].tile([P, 2048], F32, name="e", tag=slot[1], align_bytes=64)
+            def new_half_row():
+                place = half_row_places.pop(0)
+                half_row_places.append(place)
+                return place[0].tile([P, 4 * WIDE], F32, name="half_row", tag=place[1], align_bytes=64)
 
-            def chunks_of(i):
-                if i == 31:
+            def pieces_of(i):
+                if i == ROW_TILES - 1:
                     return [(0, 1024), (1024, 1024), (2048, 1024), (3072, 512), (3584, 512)]
                 return [(0, 1024), (1024, 1024), (2048, 1024), (3072, 1024)]
 
-            def chunk_ap(i, c):
-                lo, width = chunks_of(i)[c]
-                return row_e[(i, lo // 2048)][:, lo % 2048 : lo % 2048 + width]
+            def piece(i, c):
+                first, width = pieces_of(i)[c]
+                return half_rows[(i, first // 2048)][:, first % 2048 : first % 2048 + width]
 
             def new_stats():
-                k = bump("st", 3)
-                d = {}
-                for nm_, width in (("nm", 5), ("z", 5), ("f", 5), ("fz", 5), ("nM", 1), ("Z", 1), ("r", 1)):
-                    d[nm_] = st2.tile([P, width], F32, name=nm_, tag="%s%d" % (nm_, k))
-                return d
+                tag = turn("stats", 3)
+                stats = {}
+                for name, width in (
+                    ("neg_max", 5),
+                    ("sum", 5),
+                    ("lift", 5),
+                    ("lifted", 5),
+                    ("neg_row_max", 1),
+                    ("row_sum", 1),
+                    ("inverse", 1),
+                ):
+                    stats[name] = stage.tile([P, width], F32, name=name, tag=name + tag)
+                return stats
 
-            def row_scale(i):
-                s = stats[i]
-                nc.vector.reciprocal(out=s["r"][:], in_=s["Z"][:])
-                last = i == 31
-                for c in range(len(chunks_of(i))):
-                    e = chunk_ap(i, c)
-                    eng = nc.vector if (last and c < 3) else nc.gpsimd
-                    eng.tensor_scalar(
-                        out=e,
-                        in0=e,
-                        scalar1=s["f"][:, c : c + 1],
-                        scalar2=s["r"][:, 0:1],
+            def scale_and_store(i):
+                stats = stats_of_row[i]
+                nc.vector.reciprocal(out=stats["inverse"][:], in_=stats["row_sum"][:])
+                last = i == ROW_TILES - 1
+                engine = nc.vector if last else nc.gpsimd
+                for c in range(len(pieces_of(i))):
+                    first, width = pieces_of(i)[c]
+                    engine.tensor_scalar(
+                        out=piece(i, c),
+                        in0=piece(i, c),
+                        scalar1=stats["lift"][:, c : c + 1],
+                        scalar2=stats["inverse"][:, 0:1],
                         op0=ALU.mult,
                         op1=ALU.mult,
                     )
-                    lo, width = chunks_of(i)[c]
                     if last:
-                        nc.sync.dma_start(out=out[i * P : (i + 1) * P, lo : lo + width], in_=e)
+                        nc.sync.dma_start(out=out[i * P : (i + 1) * P, first : first + width], in_=piece(i, c))
                     elif c % 2 == 1:
-                        hh = c // 2
                         nc.sync.dma_start(
-                            out=out[i * P : (i + 1) * P, 2048 * hh : 2048 * (hh + 1)], in_=row_e[(i, hh)][:]
+                            out=out[i * P : (i + 1) * P, first - 1024 : first + 1024], in_=half_rows[(i, c // 2)][:]
                         )
 
-            def row_sum(i):
-                s = stats[i]
-                nch = len(chunks_of(i))
+            def sum_row(i):
+                stats = stats_of_row[i]
+                n = len(pieces_of(i))
                 nc.vector.scalar_tensor_tensor(
-                    out=s["fz"][:, 0:nch],
-                    in0=s["f"][:, 0:nch],
+                    out=stats["lifted"][:, 0:n],
+                    in0=stats["lift"][:, 0:n],
                     scalar=1.0,
-                    in1=s["z"][:, 0:nch],
+                    in1=stats["sum"][:, 0:n],
                     op0=ALU.mult,
                     op1=ALU.mult,
-                    accum_out=s["Z"][:, 0:1],
+                    accum_out=stats["row_sum"][:, 0:1],
                 )
-                later(1, lambda: row_scale(i))
+                later(1, lambda: scale_and_store(i))
 
-            def row_min(i):
-                s = stats[i]
-                nch = len(chunks_of(i))
-                nc.vector.tensor_reduce(out=s["nM"][:], in_=s["nm"][:, 0:nch], axis=AX.X, op=ALU.min)
+            def max_of_row(i):
+                stats = stats_of_row[i]
+                n = len(pieces_of(i))
+                nc.vector.tensor_reduce(out=stats["neg_row_max"][:], in_=stats["neg_max"][:, 0:n], axis=AX.X, op=ALU.min)
                 nc.scalar.activation(
-                    out=s["f"][:, 0:nch], in_=s["nm"][:, 0:nch], func=ACT.Exp, bias=s["nM"][:, 0:1], scale=-1.0
+                    out=stats["lift"][:, 0:n],
+                    in_=stats["neg_max"][:, 0:n],
+                    func=ACT.Exp,
+                    bias=stats["neg_row_max"][:, 0:1],
+                    scale=-1.0,
                 )
-                later(1, lambda: row_sum(i))
+                later(1, lambda: sum_row(i))
 
-            def chunk_min(i, c):
-                s = stats[i]
-                e = chunk_ap(i, c)
-                nc.vector.tensor_reduce(out=s["nm"][:, c : c + 1], in_=e, axis=AX.X, op=ALU.min)
+            def exp_of_piece(i, c):
+                stats = stats_of_row[i]
+                nc.vector.tensor_reduce(out=stats["neg_max"][:, c : c + 1], in_=piece(i, c), axis=AX.X, op=ALU.min)
                 nc.scalar.activation(
-                    out=e, in_=e, func=ACT.Exp, bias=s["nm"][:, c : c + 1], scale=-1.0, accum_out=s["z"][:, c : c + 1]
+                    out=piece(i, c),
+                    in_=piece(i, c),
+                    func=ACT.Exp,
+                    bias=stats["neg_max"][:, c : c + 1],
+                    scale=-1.0,
+                    accum_out=stats["sum"][:, c : c + 1],
                 )
-                if c == len(chunks_of(i)) - 1:
-                    later(1, lambda: row_min(i))
+                if c == len(pieces_of(i)) - 1:
+                    later(1, lambda: max_of_row(i))
 
             def mask(i, j, bank):
                 if j == 0:
-                    stats[i] = new_stats()
+                    stats_of_row[i] = new_stats()
                 if j % 4 == 0:
-                    row_e[(i, j // 4)] = new_e()
-                e = row_e[(i, j // 4)]
+                    half_rows[(i, j // 4)] = new_half_row()
                 nc.vector.scalar_tensor_tensor(
-                    out=e[:, (j % 4) * 512 : (j % 4) * 512 + 512],
+                    out=half_rows[(i, j // 4)][:, (j % 4) * WIDE : (j % 4 + 1) * WIDE],
                     in0=bank[:],
                     scalar=-1.0,
-                    in1=adj_t[i][:, j * 512 : (j + 1) * 512],
+                    in1=adj_of_row[i][:, j * WIDE : (j + 1) * WIDE],
                     op0=ALU.mult,
                     op1=ALU.mult,
                 )
-                if j == 7:
+                if j == BANKS - 1:
                     load_adj(i + 2)
-                ends = [lo + width for lo, width in chunks_of(i)]
-                if (j + 1) * 512 in ends:
-                    later(1, lambda: chunk_min(i, ends.index((j + 1) * 512)))
+                ends = [first + width for first, width in pieces_of(i)]
+                if (j + 1) * WIDE in ends:
+                    later(1, lambda: exp_of_piece(i, ends.index((j + 1) * WIDE)))
 
             def score_job(i, j):
-                b = i // 4
-                r = i % 4
-                qcodes, qscales = qt[b]
-                bank = new_bank([P, 512])
-                for G in range(4):
+                codes, scales = q_of_block[i // 4]
+                rows = ((i % 4) * P, (i % 4 + 1) * P)
+                bank = new_bank([P, WIDE])
+                for c in range(GROUPS):
                     nc.tensor.matmul_mx(
                         out=bank[:],
-                        lhsT=qcodes[:, G, r * P : (r + 1) * P].bitcast(FP8X4),
-                        lhsT_scale=qscales[G][4 * G :, r * P : (r + 1) * P],
-                        rhs=kc[G][:, j * 512 : (j + 1) * 512].bitcast(FP8X4),
-                        rhs_scale=ks[4 * G :, j * 512 : (j + 1) * 512],
-                        start=(G == 0),
-                        stop=(G == 3),
+                        lhsT=codes[:, c, rows[0] : rows[1]].bitcast(FP8X4),
+                        lhsT_scale=scales[4 * c :, rows[0] : rows[1]],
+                        rhs=k_codes[c][:, j * WIDE : (j + 1) * WIDE].bitcast(FP8X4),
+                        rhs_scale=k_scales[4 * c :, j * WIDE : (j + 1) * WIDE],
+                        start=(c == 0),
+                        stop=(c == GROUPS - 1),
                     )
                 later(1, lambda: mask(i, j, bank))
                 tick()
 
-            def finish_unit2(raw, codes_ap, scales_ap):
-                def step2(grp):
-                    nc.vector.quantize_mx(out=codes_ap, scales=scales_ap, in_=grp[:])
-
-                def step1():
-                    grp = st2.tile([P, 2048], BF16, name="og", tag="og", align_bytes=64)
+            def after_q_unit(raw, codes, scales):
+                def interleave():
+                    grouped = stage.tile([P, 4 * WIDE], BF16, name="grouped", tag="grouped", align_bytes=64)
                     nc.scalar.copy(
-                        out=grp[:].rearrange("p (n t) -> p n t", t=4), in_=raw[:].rearrange("p t n -> p n t")
+                        out=grouped[:].rearrange("p (n t) -> p n t", t=4), in_=raw[:].rearrange("p t n -> p n t")
                     )
-                    later(4, lambda: step2(grp))
+                    later(4, lambda: nc.vector.quantize_mx(out=codes, scales=scales, in_=grouped[:]))
 
-                later(1, step1)
+                later(1, interleave)
 
             load_adj(1)
-            qraw = {}
-            for b in range(NB):
+            for b in range(BLOCKS):
                 if b >= 1:
-                    efree.insert(0, (keep, "h%d" % b))
-                todo = []
-                if b + 1 < NB:
-                    for G in range(4):
+                    half_row_places.insert(0, (keep, "h%d" % b))
+                q_jobs = []
+                if b + 1 < BLOCKS:
+                    q_of_block[b + 1] = codes_at(Q_PLACE[(b + 1) % 2])
+                    for c in range(GROUPS):
                         for t in range(4):
-                            todo.append((G, t))
-                for s in range(32):
-                    n_q = 0
-                    if s == 0:
-                        n_q = 4
-                    elif s % 2 == 0 and s <= 24:
-                        n_q = 1
-                    for k in range(n_q):
-                        if len(todo) > 0:
-                            G, t = todo.pop(0)
-                            if G == 0 and t == 0:
-                                qt[b + 1] = code_tile(2 + (b + 1) % 2)
-                            if t == 0:
-                                qraw[0] = st2.tile([P, 4, 512], BF16, name="qraw", tag="qraw")
-                            proj_job(wt[4 + G], b + 1, t, qraw[0], qb32[:, 4 * G + t : 4 * G + t + 1])
-                            if t == 3:
-                                finish_unit2(
-                                    qraw[0], qt[b + 1][0][:, G, :].bitcast(FP8X4), qt[b + 1][1][G][4 * G :, :]
-                                )
-                    score_job(4 * b + s // 8, s % 8)
-            flush()
+                            q_jobs.append((c, t))
+                raw = None
+                for s in range(4 * BANKS):
+                    due = 4 if s == 0 else (1 if s % 2 == 0 else 0)
+                    for count in range(min(due, len(q_jobs))):
+                        c, t = q_jobs.pop(0)
+                        if t == 0:
+                            raw = stage.tile([P, 4, WIDE], BF16, name="raw", tag="raw")
+                        projection_job(GROUPS + c, b + 1, t, raw, q_bias)
+                        if t == 3:
+                            codes, scales = q_of_block[b + 1]
+                            after_q_unit(raw, codes[:, c, :].bitcast(FP8X4), scales[4 * c :, :])
+                    score_job(4 * b + s // BANKS, s % BANKS)
+            run_out()

from contextlib import ExitStack

import concourse.mybir as mybir
from concourse.masks import make_identity

F32 = mybir.dt.float32
BF16 = mybir.dt.bfloat16
U32 = mybir.dt.uint32
U8 = mybir.dt.uint8
FP8X4 = mybir.dt.float8_e4m3fn_x4
ACT = mybir.ActivationFunctionType
ALU = mybir.AluOpType
AX = mybir.AxisListType

P = 128
TOKENS = 4096
FEATURES = 2048
PASSES = FEATURES // (4 * P)
WIDE = 512
BLOCKS = TOKENS // WIDE
GROUPS = FEATURES // WIDE
ROW_TILES = TOKENS // P
BANKS = 8

FLOPS = 2 * 2 * TOKENS * FEATURES * FEATURES + 2 * TOKENS * TOKENS * FEATURES

WEIGHT_PLACE = [0, 1, 2, 3, 4, 5, 0, 1]
Q_PLACE = [2, 3]
WEIGHT_TASKS = 2 * GROUPS * PASSES


def tile_gtransformerblock_pb_l_kernel(tc, h, adj, Qw, Qb, Kw, Kb, out):
    nc = tc.nc

    clock = [0]
    entered = {}
    turns = {}

    def later(lag, step):
        due = clock[0] + lag
        if due not in entered:
            entered[due] = []
        entered[due].append(step)

    def tick():
        while clock[0] in entered:
            for step in entered.pop(clock[0]):
                step()
        clock[0] += 1

    def run_out():
        while len(entered) > 0:
            tick()

    def turn(family, n):
        count = turns.get(family, 0)
        turns[family] = count + 1
        return "%s%d" % (family, count % n)

    with ExitStack() as ctx:
        ctx.enter_context(tc.manual_schedule())
        keep = ctx.enter_context(tc.tile_pool(name="keep", bufs=1))
        psum = ctx.enter_context(tc.psum_pool(name="psum", bufs=1))

        def new_bank(shape):
            return psum.tile(shape, F32, name="bank", tag=turn("bank", BANKS))

        def codes_at(place):
            codes = keep.tile([P, PASSES, WIDE], U32, name="codes", tag="codes%d" % place, align_bytes=64)
            scales = keep.tile([P, WIDE], U8, name="scales", tag="scales%d" % place, align_bytes=64)
            return (codes, scales)

        k_codes = []
        for c in range(GROUPS):
            k_codes.append(keep.tile([P, TOKENS], U32, name="k_codes", tag="k_codes%d" % c, align_bytes=64))
        k_scales = keep.tile([P, TOKENS], U8, name="k_scales", tag="k_scales", align_bytes=64)
        h_codes = []
        h_scales = []
        for b in range(BLOCKS):
            h_codes.append(keep.tile([P, PASSES, WIDE], U32, name="h_codes", tag="h%d" % b, align_bytes=64))
            h_scales.append(keep.tile([P, WIDE], U8, name="h_scales", tag="h_scales%d" % b, align_bytes=64))
        weights = {}
        for n in range(6):
            weights[n] = codes_at(WEIGHT_PLACE[n])
        k_bias = keep.tile([P, GROUPS * 4], F32, name="k_bias", tag="k_bias")
        q_bias = keep.tile([P, GROUPS * 4], F32, name="q_bias", tag="q_bias")
        q_of_block = {}
        adj_of_row = {}

        def projection_job(n, b, t, raw, bias):
            codes, scales = weights[n]
            bank = new_bank([P, WIDE])
            for g in range(PASSES):
                nc.tensor.matmul_mx(
                    out=bank[:],
                    lhsT=codes[:, g, t * P : (t + 1) * P].bitcast(FP8X4),
                    lhsT_scale=scales[4 * g :, t * P : (t + 1) * P],
                    rhs=h_codes[b][:, g, :].bitcast(FP8X4),
                    rhs_scale=h_scales[b][4 * g :, :],
                    start=(g == 0),
                    stop=(g == PASSES - 1),
                )
            column = 4 * (n % GROUPS) + t
            later(
                1,
                lambda: nc.scalar.activation(
                    out=raw[:, t, :], in_=bank[:], func=ACT.Identity, bias=bias[:, column : column + 1], scale=1.0
                ),
            )
            tick()

        with tc.tile_pool(name="phase1", bufs=1) as stage:
            identity = stage.tile([P, P], F32, name="identity", tag="identity")
            make_identity(nc, identity[:])

            zero = stage.tile([P, 1], F32, name="zero", tag="zero")
            one = stage.tile([P, 1], F32, name="one", tag="one")
            nc.vector.memset(zero[:], 0.0)
            nc.scalar.activation(out=one[:], in_=zero[:], func=ACT.Exp)

            k_bias16 = stage.tile([P, GROUPS, 4], BF16, name="k_bias16", tag="k_bias16")
            q_bias16 = stage.tile([P, GROUPS, 4], BF16, name="q_bias16", tag="q_bias16")
            nc.scalar.dma_start(out=k_bias16[:], in_=Kb.rearrange("(c p t) -> p c t", p=P, t=4))
            nc.scalar.dma_start(out=q_bias16[:], in_=Qb.rearrange("(c p t) -> p c t", p=P, t=4))

            h_rows = {}
            w_rows = {}

            def load_h(b, half):
                if b < BLOCKS:
                    for r in range(2):
                        first = (4 * b + 2 * half + r) * P
                        rows = stage.tile([P, FEATURES], BF16, name="h_rows", tag="h_rows%d" % (2 * half + r))
                        nc.sync.dma_start(out=rows[:], in_=h[first : first + P, :])
                        h_rows[(b, half, r)] = rows

            def new_grouped():
                return stage.tile([P, 4 * WIDE], BF16, name="grouped", tag=turn("grouped", 3), align_bytes=64)

            def load_weights(w):
                if w < WEIGHT_TASKS:
                    source = Kw if w < WEIGHT_TASKS // 2 else Qw
                    c = (w // PASSES) % GROUPS
                    g = w % PASSES
                    rows = stage.tile([P, 4, WIDE], BF16, name="w_rows", tag="w_rows%d" % (w % 2))
                    nc.sync.dma_start(
                        out=rows[:],
                        in_=source[4 * P * g : 4 * P * (g + 1), WIDE * c : WIDE * (c + 1)].rearrange(
                            "(p j) c -> p j c", j=4
                        ),
                    )
                    w_rows[w] = rows

            def sort_weights(w, on_scalar):
                grouped = new_grouped()
                target = grouped[:].rearrange("p (t m j) -> p t m j", t=4, j=4)
                source = w_rows.pop(w)[:].rearrange("p j (m t) -> p t m j", t=4)
                if on_scalar:
                    nc.scalar.copy(out=target, in_=source)
                else:
                    nc.vector.tensor_copy(out=target, in_=source)
                load_weights(w + 2)
                return grouped

            def quantise_weights(w, grouped):
                n = w // PASSES
                g = w % PASSES
                if n not in weights:
                    weights[n] = codes_at(WEIGHT_PLACE[n])
                codes, scales = weights[n]
                nc.vector.quantize_mx(out=codes[:, g, :].bitcast(FP8X4), scales=scales[4 * g :, :], in_=grouped[:])

            def transpose_job(b, half, g):
                bank = new_bank([P, 2, 2 * P])
                for r in range(2):
                    words = h_rows[(b, half, r)][:].bitcast(F32)
                    for u in range(2):
                        nc.tensor.transpose(
                            bank[:, u, r * P : (r + 1) * P], words[:, 2 * P * g + u : 2 * P * (g + 1) : 2], identity[:]
                        )

                def quantise(grouped):
                    tokens = (2 * P * half, 2 * P * (half + 1))
                    nc.vector.quantize_mx(
                        out=h_codes[b][:, g, tokens[0] : tokens[1]].bitcast(FP8X4),
                        scales=h_scales[b][4 * g :, tokens[0] : tokens[1]],
                        in_=grouped[:].rearrange("p r j -> p (r j)"),
                    )

                def empty():
                    grouped = stage.tile([P, 2 * P, 4], BF16, name="h_grouped", tag=turn("h_grouped", 2), align_bytes=64)
                    nc.scalar.copy(out=grouped[:].bitcast(F32), in_=bank[:].rearrange("p u r -> p r u"))
                    later(1, lambda: quantise(grouped))

                later(1, empty)
                tick()

            def transpose_half(b, half):
                if b < BLOCKS:
                    for g in range(PASSES):
                        transpose_job(b, half, g)
                    load_h(b + 1, half)

            def after_unit(raw, codes, scales, w):
                def interleave():
                    grouped = new_grouped()
                    nc.vector.tensor_copy(
                        out=grouped[:].rearrange("p (n t) -> p n t", t=4), in_=raw[:].rearrange("p t n -> p n t")
                    )
                    later(1, lambda: nc.vector.quantize_mx(out=codes, scales=scales, in_=grouped[:]))
                    if w < WEIGHT_TASKS:
                        on_scalar = w >= 4 + BLOCKS and w % 2 == 1
                        w_grouped = sort_weights(w, on_scalar)
                        later(3 if on_scalar else 1, lambda: quantise_weights(w, w_grouped))

                later(1, interleave)

            load_h(0, 0)
            load_weights(0)
            load_weights(1)
            load_h(0, 1)
            for half in range(2):
                first_grouped = sort_weights(2 * half, False)
                second_grouped = sort_weights(2 * half + 1, False)
                quantise_weights(2 * half, first_grouped)
                transpose_half(0, half)
                quantise_weights(2 * half + 1, second_grouped)
            run_out()
            nc.vector.tensor_copy(out=k_bias[:], in_=k_bias16[:].rearrange("p c t -> p (c t)"))
            nc.vector.tensor_copy(out=q_bias[:], in_=q_bias16[:].rearrange("p c t -> p (c t)"))

            units = []
            for n in range(GROUPS):
                for b in range(BLOCKS):
                    units.append((n, b))
            for c in range(GROUPS):
                units.append((GROUPS + c, 0))
            for number, (n, b) in enumerate(units):
                raw = stage.tile([P, 4, WIDE], BF16, name="raw", tag=turn("raw", 2))
                for t in range(4):
                    if n == 0 and t % 2 == 0:
                        transpose_half(b + 1, t // 2)
                    projection_job(n, b, t, raw, k_bias if n < GROUPS else q_bias)
                if n < GROUPS:
                    codes = k_codes[n][:, WIDE * b : WIDE * (b + 1)]
                    scales = k_scales[4 * n :, WIDE * b : WIDE * (b + 1)]
                else:
                    if 0 not in q_of_block:
                        q_of_block[0] = codes_at(Q_PLACE[0])
                    codes = q_of_block[0][0][:, n - GROUPS, :]
                    scales = q_of_block[0][1][4 * (n - GROUPS) :, :]
                after_unit(raw, codes.bitcast(FP8X4), scales, 4 + number)

            adj_of_row[0] = keep.tile([P, TOKENS], BF16, name="adj_rows", tag="h0", align_bytes=64)
            nc.sync.dma_start(out=adj_of_row[0][:], in_=adj[0:P, :])
            run_out()

        with tc.tile_pool(name="phase2", bufs=1) as stage:
            half_row_places = [(stage, "half0"), (stage, "half1"), (stage, "half2"), (stage, "half3")]
            half_rows = {}
            stats_of_row = {}

            def load_adj(i):
                if i < ROW_TILES:
                    if i % 2 == 0:
                        rows = keep.tile([P, TOKENS], BF16, name="adj_rows", tag="h0", align_bytes=64)
                    else:
                        rows = stage.tile([P, TOKENS], BF16, name="adj_rows", tag="adj_odd", align_bytes=64)
                    nc.sync.dma_start(out=rows[:], in_=adj[i * P : (i + 1) * P, :])
                    adj_of_row[i] = rows

            def new_half_row():
                place = half_row_places.pop(0)
                half_row_places.append(place)
                return place[0].tile([P, 4 * WIDE], F32, name="half_row", tag=place[1], align_bytes=64)

            def pieces_of(i):
                if i == ROW_TILES - 1:
                    return [(0, 1024), (1024, 1024), (2048, 1024), (3072, 512), (3584, 512)]
                return [(0, 1024), (1024, 1024), (2048, 1024), (3072, 1024)]

            def piece(i, c):
                first, width = pieces_of(i)[c]
                return half_rows[(i, first // 2048)][:, first % 2048 : first % 2048 + width]

            def new_stats():
                tag = turn("stats", 3)
                stats = {}
                for name, width in (
                    ("neg_max", 5),
                    ("sum", 5),
                    ("lift", 5),
                    ("lifted", 5),
                    ("neg_row_max", 1),
                    ("row_sum", 1),
                    ("inverse", 1),
                ):
                    stats[name] = stage.tile([P, width], F32, name=name, tag=name + tag)
                return stats

            def scale_and_store(i):
                stats = stats_of_row[i]
                nc.vector.reciprocal(out=stats["inverse"][:], in_=stats["row_sum"][:])
                last = i == ROW_TILES - 1
                engine = nc.vector if last else nc.gpsimd
                for c in range(len(pieces_of(i))):
                    first, width = pieces_of(i)[c]
                    engine.tensor_scalar(
                        out=piece(i, c),
                        in0=piece(i, c),
                        scalar1=stats["lift"][:, c : c + 1],
                        scalar2=stats["inverse"][:, 0:1],
                        op0=ALU.mult,
                        op1=ALU.mult,
                    )
                    if last:
                        nc.sync.dma_start(out=out[i * P : (i + 1) * P, first : first + width], in_=piece(i, c))
                    elif c % 2 == 1:
                        nc.sync.dma_start(
                            out=out[i * P : (i + 1) * P, first - 1024 : first + 1024], in_=half_rows[(i, c // 2)][:]
                        )

            def sum_row(i):
                stats = stats_of_row[i]
                n = len(pieces_of(i))
                nc.vector.scalar_tensor_tensor(
                    out=stats["lifted"][:, 0:n],
                    in0=stats["lift"][:, 0:n],
                    scalar=1.0,
                    in1=stats["sum"][:, 0:n],
                    op0=ALU.mult,
                    op1=ALU.mult,
                    accum_out=stats["row_sum"][:, 0:1],
                )
                later(1, lambda: scale_and_store(i))

            def max_of_row(i):
                stats = stats_of_row[i]
                n = len(pieces_of(i))
                nc.vector.tensor_reduce(out=stats["neg_row_max"][:], in_=stats["neg_max"][:, 0:n], axis=AX.X, op=ALU.min)
                nc.scalar.activation(
                    out=stats["lift"][:, 0:n],
                    in_=stats["neg_max"][:, 0:n],
                    func=ACT.Exp,
                    bias=stats["neg_row_max"][:, 0:1],
                    scale=-1.0,
                )
                later(1, lambda: sum_row(i))

            def exp_of_piece(i, c):
                stats = stats_of_row[i]
                nc.vector.tensor_reduce(out=stats["neg_max"][:, c : c + 1], in_=piece(i, c), axis=AX.X, op=ALU.min)
                nc.scalar.activation(
                    out=piece(i, c),
                    in_=piece(i, c),
                    func=ACT.Exp,
                    bias=stats["neg_max"][:, c : c + 1],
                    scale=-1.0,
                    accum_out=stats["sum"][:, c : c + 1],
                )
                if c == len(pieces_of(i)) - 1:
                    later(1, lambda: max_of_row(i))

            def mask(i, j, bank):
                if j == 0:
                    stats_of_row[i] = new_stats()
                if j % 4 == 0:
                    half_rows[(i, j // 4)] = new_half_row()
                nc.vector.scalar_tensor_tensor(
                    out=half_rows[(i, j // 4)][:, (j % 4) * WIDE : (j % 4 + 1) * WIDE],
                    in0=bank[:],
                    scalar=-1.0,
                    in1=adj_of_row[i][:, j * WIDE : (j + 1) * WIDE],
                    op0=ALU.mult,
                    op1=ALU.mult,
                )
                if j == BANKS - 1:
                    load_adj(i + 2)
                ends = [first + width for first, width in pieces_of(i)]
                if (j + 1) * WIDE in ends:
                    later(1, lambda: exp_of_piece(i, ends.index((j + 1) * WIDE)))

            def score_job(i, j):
                codes, scales = q_of_block[i // 4]
                rows = ((i % 4) * P, (i % 4 + 1) * P)
                bank = new_bank([P, WIDE])
                for c in range(GROUPS):
                    nc.tensor.matmul_mx(
                        out=bank[:],
                        lhsT=codes[:, c, rows[0] : rows[1]].bitcast(FP8X4),
                        lhsT_scale=scales[4 * c :, rows[0] : rows[1]],
                        rhs=k_codes[c][:, j * WIDE : (j + 1) * WIDE].bitcast(FP8X4),
                        rhs_scale=k_scales[4 * c :, j * WIDE : (j + 1) * WIDE],
                        start=(c == 0),
                        stop=(c == GROUPS - 1),
                    )
                later(1, lambda: mask(i, j, bank))
                tick()

            def after_q_unit(raw, codes, scales):
                def interleave():
                    grouped = stage.tile([P, 4 * WIDE], BF16, name="grouped", tag="grouped", align_bytes=64)
                    nc.scalar.copy(
                        out=grouped[:].rearrange("p (n t) -> p n t", t=4), in_=raw[:].rearrange("p t n -> p n t")
                    )
                    later(4, lambda: nc.vector.quantize_mx(out=codes, scales=scales, in_=grouped[:]))

                later(1, interleave)

            load_adj(1)
            for b in range(BLOCKS):
                if b >= 1:
                    half_row_places.insert(0, (keep, "h%d" % b))
                q_jobs = []
                if b + 1 < BLOCKS:
                    q_of_block[b + 1] = codes_at(Q_PLACE[(b + 1) % 2])
                    for c in range(GROUPS):
                        for t in range(4):
                            q_jobs.append((c, t))
                raw = None
                for s in range(4 * BANKS):
                    due = 4 if s == 0 else (1 if s % 2 == 0 else 0)
                    for count in range(min(due, len(q_jobs))):
                        c, t = q_jobs.pop(0)
                        if t == 0:
                            raw = stage.tile([P, 4, WIDE], BF16, name="raw", tag="raw")
                        projection_job(GROUPS + c, b + 1, t, raw, q_bias)
                        if t == 3:
                            codes, scales = q_of_block[b + 1]
                            after_q_unit(raw, codes[:, c, :].bitcast(FP8X4), scales[4 * c :, :])
                    score_job(4 * b + s // BANKS, s % BANKS)
            run_out()
